import numpy as np
import ml_dtypes

BF16 = ml_dtypes.bfloat16


def bf(x):
    return np.asarray(x, np.float32).astype(BF16)


def f32(x):
    return np.asarray(x, np.float32)


def f64(x):
    return np.asarray(x).astype(np.float64)


def striped(idx):
    return np.tile(idx.reshape(-1, 16).T, (8, 1))


D, S, N = 512, 1024, 512
HALF = 0.5


def scaled_cols(a):
    return a * (np.sqrt(D) / np.sqrt(np.sum(a * a, axis=0, keepdims=True)))


def setup_inputs():
    means = f32(scaled_cols(np.random.uniform(-1.0, 1.0, (D, S))))
    feat = f32(scaled_cols(np.random.standard_normal((D, N))))
    return {"means": means, "feat": feat, "offs": striped(np.random.permutation(np.tile(np.arange(S), 2))[:N])}


def reference(means, feat, offs):
    idx = offs[:16].T.reshape(-1)
    nf = -f64(feat)
    diff = f64(means)[:, idx] + nf
    return HALF * diff * diff

@@ -1,0 +1,48 @@
+import math
+
+import concourse.mybir as mybir
+
+F32 = mybir.dt.float32
+U16 = mybir.dt.uint16
+ADD = mybir.AluOpType.add
+COPY = mybir.ActivationFunctionType.Copy
+SQUARE = mybir.ActivationFunctionType.Square
+
+P = 128
+
+
+def tile_ltloss_kernel(tc, means, feat, offs, out):
+    nc = tc.nc
+    n_features, n_classes = means.shape
+    n_samples = feat.shape[1]
+    n_blocks = n_features // P
+
+    with (
+        tc.tile_pool(name="held", bufs=1) as held,
+        tc.tile_pool(name="blocks", bufs=n_blocks) as blocks,
+    ):
+        offsets = held.tile([P, n_samples // 16], U16, name="offsets")
+        nc.sync.dma_start(offsets[:], offs)
+
+        def load_block(b):
+            rows = slice(b * P, (b + 1) * P)
+            samples = blocks.tile([P, n_samples], F32, name="samples")
+            nc.sync.dma_start(samples[:], feat[rows, :])
+            window = blocks.tile([P, n_classes], F32, name="window")
+            nc.sync.dma_start(window[:], means[rows, :])
+            negated = blocks.tile([P, n_samples], F32, name="negated")
+            nc.scalar.activation(negated[:], samples[:], COPY, scale=-1.0)
+            return window, negated
+
+        loaded = load_block(0)
+        for b in range(n_blocks):
+            window, negated = loaded
+            if b + 1 < n_blocks:
+                loaded = load_block(b + 1)
+
+            diff = blocks.tile([P, n_samples], F32, name="diff")
+            nc.vector.tensor_tensor(diff[:], window[:].indirect(offsets[:]), negated[:], ADD)
+
+            loss = blocks.tile([P, n_samples], F32, name="loss")
+            nc.scalar.activation(loss[:], diff[:], SQUARE, scale=math.sqrt(0.5))
+            nc.scalar.dma_start(out[b * P : (b + 1) * P, :], loss[:])

@@ -45,4 +45,4 @@ def tile_ltloss_kernel(tc, means, feat, offs, out):
 
             loss = blocks.tile([P, n_samples], F32, name="loss")
             nc.scalar.activation(loss[:], diff[:], SQUARE, scale=math.sqrt(0.5))
-            nc.scalar.dma_start(out[b * P : (b + 1) * P, :], loss[:])
+            nc.sync.dma_start(out[b * P : (b + 1) * P, :], loss[:])

@@ -9,6 +9,7 @@ COPY = mybir.ActivationFunctionType.Copy
 SQUARE = mybir.ActivationFunctionType.Square
 
 P = 128
+N_PIECES = 2
 
 
 def tile_ltloss_kernel(tc, means, feat, offs, out):
@@ -16,10 +17,12 @@ def tile_ltloss_kernel(tc, means, feat, offs, out):
     n_features, n_classes = means.shape
     n_samples = feat.shape[1]
     n_blocks = n_features // P
+    piece = n_samples // N_PIECES
 
     with (
         tc.tile_pool(name="held", bufs=1) as held,
         tc.tile_pool(name="blocks", bufs=n_blocks) as blocks,
+        tc.tile_pool(name="pieces", bufs=n_blocks * N_PIECES) as pieces,
     ):
         offsets = held.tile([P, n_samples // 16], U16, name="offsets")
         nc.sync.dma_start(offsets[:], offs)
@@ -40,9 +43,13 @@ def tile_ltloss_kernel(tc, means, feat, offs, out):
             if b + 1 < n_blocks:
                 loaded = load_block(b + 1)
 
-            diff = blocks.tile([P, n_samples], F32, name="diff")
-            nc.vector.tensor_tensor(diff[:], window[:].indirect(offsets[:]), negated[:], ADD)
+            for first in range(0, n_samples, piece):
+                cols = slice(first, first + piece)
+                picked = window[:].indirect(offsets[:, first // 16 : (first + piece) // 16])
 
-            loss = blocks.tile([P, n_samples], F32, name="loss")
-            nc.scalar.activation(loss[:], diff[:], SQUARE, scale=math.sqrt(0.5))
-            nc.sync.dma_start(out[b * P : (b + 1) * P, :], loss[:])
+                diff = pieces.tile([P, piece], F32, name="diff")
+                nc.vector.tensor_tensor(diff[:], picked, negated[:, cols], ADD)
+
+                loss = pieces.tile([P, piece], F32, name="loss")
+                nc.scalar.activation(loss[:], diff[:], SQUARE, scale=math.sqrt(0.5))
+                nc.scalar.dma_start(out[b * P : (b + 1) * P, cols], loss[:])

@@ -9,7 +9,7 @@ COPY = mybir.ActivationFunctionType.Copy
 SQUARE = mybir.ActivationFunctionType.Square
 
 P = 128
-N_PIECES = 2
+LAST_PIECES = 2
 
 
 def tile_ltloss_kernel(tc, means, feat, offs, out):
@@ -17,12 +17,11 @@ def tile_ltloss_kernel(tc, means, feat, offs, out):
     n_features, n_classes = means.shape
     n_samples = feat.shape[1]
     n_blocks = n_features // P
-    piece = n_samples // N_PIECES
 
     with (
         tc.tile_pool(name="held", bufs=1) as held,
         tc.tile_pool(name="blocks", bufs=n_blocks) as blocks,
-        tc.tile_pool(name="pieces", bufs=n_blocks * N_PIECES) as pieces,
+        tc.tile_pool(name="pieces", bufs=n_blocks - 1 + LAST_PIECES) as pieces,
     ):
         offsets = held.tile([P, n_samples // 16], U16, name="offsets")
         nc.sync.dma_start(offsets[:], offs)
@@ -43,6 +42,7 @@ def tile_ltloss_kernel(tc, means, feat, offs, out):
             if b + 1 < n_blocks:
                 loaded = load_block(b + 1)
 
+            piece = n_samples // (LAST_PIECES if b == n_blocks - 1 else 1)
             for first in range(0, n_samples, piece):
                 cols = slice(first, first + piece)
                 picked = window[:].indirect(offsets[:, first // 16 : (first + piece) // 16])

@@ -5,10 +5,10 @@ import concourse.mybir as mybir
 F32 = mybir.dt.float32
 U16 = mybir.dt.uint16
 ADD = mybir.AluOpType.add
-COPY = mybir.ActivationFunctionType.Copy
 SQUARE = mybir.ActivationFunctionType.Square
 
 P = 128
+PAIR = 2
 LAST_PIECES = 2
 
 
@@ -18,6 +18,10 @@ def tile_ltloss_kernel(tc, means, feat, offs, out):
     n_samples = feat.shape[1]
     n_blocks = n_features // P
 
+    means_blocks = means.rearrange("(p b) c -> p b c", b=n_blocks)
+    feat_blocks = feat.rearrange("(p b) j -> p (b j)", b=n_blocks)
+    out_blocks = out.rearrange("(p b) j -> p (b j)", b=n_blocks)
+
     with (
         tc.tile_pool(name="held", bufs=1) as held,
         tc.tile_pool(name="blocks", bufs=n_blocks) as blocks,
@@ -26,30 +30,29 @@ def tile_ltloss_kernel(tc, means, feat, offs, out):
         offsets = held.tile([P, n_samples // 16], U16, name="offsets")
         nc.sync.dma_start(offsets[:], offs)
 
-        def load_block(b):
-            rows = slice(b * P, (b + 1) * P)
-            samples = blocks.tile([P, n_samples], F32, name="samples")
-            nc.sync.dma_start(samples[:], feat[rows, :])
-            window = blocks.tile([P, n_classes], F32, name="window")
-            nc.sync.dma_start(window[:], means[rows, :])
-            negated = blocks.tile([P, n_samples], F32, name="negated")
-            nc.scalar.activation(negated[:], samples[:], COPY, scale=-1.0)
-            return window, negated
+        samples_of = []
+        windows = []
+        for first_block in range(0, n_blocks, PAIR):
+            samples = blocks.tile([P, PAIR * n_samples], F32, name="samples")
+            nc.sync.dma_start(samples[:], feat_blocks[:, first_block * n_samples : (first_block + PAIR) * n_samples])
+            for k in range(PAIR):
+                samples_of.append(samples[:, k * n_samples : (k + 1) * n_samples])
+                window = blocks.tile([P, n_classes], F32, name="window")
+                nc.sync.dma_start(window[:], means_blocks[:, first_block + k, :])
+                windows.append(window)
 
-        loaded = load_block(0)
         for b in range(n_blocks):
-            window, negated = loaded
-            if b + 1 < n_blocks:
-                loaded = load_block(b + 1)
+            negated = blocks.tile([P, n_samples], F32, name="negated")
+            nc.vector.tensor_scalar_mul(negated[:], samples_of[b], -1.0)
 
             piece = n_samples // (LAST_PIECES if b == n_blocks - 1 else 1)
             for first in range(0, n_samples, piece):
-                cols = slice(first, first + piece)
-                picked = window[:].indirect(offsets[:, first // 16 : (first + piece) // 16])
+                picked = windows[b][:].indirect(offsets[:, first // 16 : (first + piece) // 16])
 
                 diff = pieces.tile([P, piece], F32, name="diff")
-                nc.vector.tensor_tensor(diff[:], picked, negated[:, cols], ADD)
+                nc.vector.tensor_tensor(diff[:], picked, negated[:, first : first + piece], ADD)
 
                 loss = pieces.tile([P, piece], F32, name="loss")
                 nc.scalar.activation(loss[:], diff[:], SQUARE, scale=math.sqrt(0.5))
-                nc.scalar.dma_start(out[b * P : (b + 1) * P, cols], loss[:])
+                at = b * n_samples + first
+                nc.sync.dma_start(out_blocks[:, at : at + piece], loss[:])

@@ -9,6 +9,7 @@ SQUARE = mybir.ActivationFunctionType.Square
 
 P = 128
 PAIR = 2
+DMA_ALIGN = 256
 LAST_PIECES = 2
 
 
@@ -33,11 +34,11 @@ def tile_ltloss_kernel(tc, means, feat, offs, out):
         samples_of = []
         windows = []
         for first_block in range(0, n_blocks, PAIR):
-            samples = blocks.tile([P, PAIR * n_samples], F32, name="samples")
+            samples = blocks.tile([P, PAIR * n_samples], F32, name="samples", align_bytes=DMA_ALIGN)
             nc.sync.dma_start(samples[:], feat_blocks[:, first_block * n_samples : (first_block + PAIR) * n_samples])
             for k in range(PAIR):
                 samples_of.append(samples[:, k * n_samples : (k + 1) * n_samples])
-                window = blocks.tile([P, n_classes], F32, name="window")
+                window = blocks.tile([P, n_classes], F32, name="window", align_bytes=DMA_ALIGN)
                 nc.sync.dma_start(window[:], means_blocks[:, first_block + k, :])
                 windows.append(window)
 
@@ -52,7 +53,7 @@ def tile_ltloss_kernel(tc, means, feat, offs, out):
                 diff = pieces.tile([P, piece], F32, name="diff")
                 nc.vector.tensor_tensor(diff[:], picked, negated[:, first : first + piece], ADD)
 
-                loss = pieces.tile([P, piece], F32, name="loss")
+                loss = pieces.tile([P, piece], F32, name="loss", align_bytes=DMA_ALIGN)
                 nc.scalar.activation(loss[:], diff[:], SQUARE, scale=math.sqrt(0.5))
                 at = b * n_samples + first
                 nc.sync.dma_start(out_blocks[:, at : at + piece], loss[:])

@@ -9,7 +9,7 @@ SQUARE = mybir.ActivationFunctionType.Square
 
 P = 128
 PAIR = 2
-DMA_ALIGN = 256
+DMA_ALIGN = 4096
 LAST_PIECES = 2
 
 

@@ -19,9 +19,9 @@ def tile_ltloss_kernel(tc, means, feat, offs, out):
     n_samples = feat.shape[1]
     n_blocks = n_features // P
 
-    means_blocks = means.rearrange("(p b) c -> p b c", b=n_blocks)
-    feat_blocks = feat.rearrange("(p b) j -> p (b j)", b=n_blocks)
-    out_blocks = out.rearrange("(p b) j -> p (b j)", b=n_blocks)
+    means_blocks = means.rearrange("(b p) c -> b p c", p=P)
+    feat_blocks = feat.rearrange("(b p) j -> p b j", p=P)
+    out_blocks = out.rearrange("(b p) j -> b p j", p=P)
 
     with (
         tc.tile_pool(name="held", bufs=1) as held,
@@ -29,17 +29,18 @@ def tile_ltloss_kernel(tc, means, feat, offs, out):
         tc.tile_pool(name="pieces", bufs=n_blocks - 1 + LAST_PIECES) as pieces,
     ):
         offsets = held.tile([P, n_samples // 16], U16, name="offsets")
-        nc.sync.dma_start(offsets[:], offs)
 
         samples_of = []
         windows = []
         for first_block in range(0, n_blocks, PAIR):
-            samples = blocks.tile([P, PAIR * n_samples], F32, name="samples", align_bytes=DMA_ALIGN)
-            nc.sync.dma_start(samples[:], feat_blocks[:, first_block * n_samples : (first_block + PAIR) * n_samples])
+            samples = blocks.tile([P, PAIR, n_samples], F32, name="samples", align_bytes=DMA_ALIGN)
+            nc.sync.dma_start(samples[:], feat_blocks[:, first_block : first_block + PAIR, :])
+            if first_block == 0:
+                nc.sync.dma_start(offsets[:], offs)
             for k in range(PAIR):
-                samples_of.append(samples[:, k * n_samples : (k + 1) * n_samples])
+                samples_of.append(samples[:, k, :])
                 window = blocks.tile([P, n_classes], F32, name="window", align_bytes=DMA_ALIGN)
-                nc.sync.dma_start(window[:], means_blocks[:, first_block + k, :])
+                nc.sync.dma_start(window[:], means_blocks[first_block + k])
                 windows.append(window)
 
         for b in range(n_blocks):
@@ -55,5 +56,4 @@ def tile_ltloss_kernel(tc, means, feat, offs, out):
 
                 loss = pieces.tile([P, piece], F32, name="loss", align_bytes=DMA_ALIGN)
                 nc.scalar.activation(loss[:], diff[:], SQUARE, scale=math.sqrt(0.5))
-                at = b * n_samples + first
-                nc.sync.dma_start(out_blocks[:, at : at + piece], loss[:])
+                nc.sync.dma_start(out_blocks[b, :, first : first + piece], loss[:])

@@ -10,7 +10,7 @@ SQUARE = mybir.ActivationFunctionType.Square
 P = 128
 PAIR = 2
 DMA_ALIGN = 4096
-LAST_PIECES = 2
+LAST_PIECES = 4
 
 
 def tile_ltloss_kernel(tc, means, feat, offs, out):

@@ -10,7 +10,7 @@ SQUARE = mybir.ActivationFunctionType.Square
 P = 128
 PAIR = 2
 DMA_ALIGN = 4096
-LAST_PIECES = 4
+HALVINGS = 2
 
 
 def tile_ltloss_kernel(tc, means, feat, offs, out):
@@ -26,7 +26,7 @@ def tile_ltloss_kernel(tc, means, feat, offs, out):
     with (
         tc.tile_pool(name="held", bufs=1) as held,
         tc.tile_pool(name="blocks", bufs=n_blocks) as blocks,
-        tc.tile_pool(name="pieces", bufs=n_blocks - 1 + LAST_PIECES) as pieces,
+        tc.tile_pool(name="pieces", bufs=n_blocks + HALVINGS) as pieces,
     ):
         offsets = held.tile([P, n_samples // 16], U16, name="offsets")
 
@@ -47,13 +47,13 @@ def tile_ltloss_kernel(tc, means, feat, offs, out):
             negated = blocks.tile([P, n_samples], F32, name="negated")
             nc.vector.tensor_scalar_mul(negated[:], samples_of[b], -1.0)
 
-            piece = n_samples // (LAST_PIECES if b == n_blocks - 1 else 1)
-            for first in range(0, n_samples, piece):
-                picked = windows[b][:].indirect(offsets[:, first // 16 : (first + piece) // 16])
+            cuts = [0] + [n_samples - (n_samples >> k) for k in range(1, HALVINGS + 1) if b == n_blocks - 1] + [n_samples]
+            for first, end in zip(cuts[:-1], cuts[1:]):
+                picked = windows[b][:].indirect(offsets[:, first // 16 : end // 16])
 
-                diff = pieces.tile([P, piece], F32, name="diff")
-                nc.vector.tensor_tensor(diff[:], picked, negated[:, first : first + piece], ADD)
+                diff = pieces.tile([P, end - first], F32, name="diff")
+                nc.vector.tensor_tensor(diff[:], picked, negated[:, first:end], ADD)
 
-                loss = pieces.tile([P, piece], F32, name="loss", align_bytes=DMA_ALIGN)
+                loss = pieces.tile([P, end - first], F32, name="loss", align_bytes=DMA_ALIGN)
                 nc.scalar.activation(loss[:], diff[:], SQUARE, scale=math.sqrt(0.5))
-                nc.sync.dma_start(out_blocks[b, :, first : first + piece], loss[:])
+                nc.sync.dma_start(out_blocks[b, :, first:end], loss[:])

@@ -56,4 +56,7 @@ def tile_ltloss_kernel(tc, means, feat, offs, out):
 
                 loss = pieces.tile([P, end - first], F32, name="loss", align_bytes=DMA_ALIGN)
                 nc.scalar.activation(loss[:], diff[:], SQUARE, scale=math.sqrt(0.5))
-                nc.sync.dma_start(out_blocks[b, :, first:end], loss[:])
+                half = n_samples // 2
+                for at in range(first, end, half):
+                    stop = min(at + half, end)
+                    nc.sync.dma_start(out_blocks[b, :, at:stop], loss[:, at - first : stop - first])

import math

import concourse.mybir as mybir

F32 = mybir.dt.float32
U16 = mybir.dt.uint16
ADD = mybir.AluOpType.add
SQUARE = mybir.ActivationFunctionType.Square

P = 128
PAIR = 2
DMA_ALIGN = 4096
HALVINGS = 2


def tile_ltloss_kernel(tc, means, feat, offs, out):
    nc = tc.nc
    n_features, n_classes = means.shape
    n_samples = feat.shape[1]
    n_blocks = n_features // P

    means_blocks = means.rearrange("(b p) c -> b p c", p=P)
    feat_blocks = feat.rearrange("(b p) j -> p b j", p=P)
    out_blocks = out.rearrange("(b p) j -> b p j", p=P)

    with (
        tc.tile_pool(name="held", bufs=1) as held,
        tc.tile_pool(name="blocks", bufs=n_blocks) as blocks,
        tc.tile_pool(name="pieces", bufs=n_blocks + HALVINGS) as pieces,
    ):
        offsets = held.tile([P, n_samples // 16], U16, name="offsets")

        samples_of = []
        windows = []
        for first_block in range(0, n_blocks, PAIR):
            samples = blocks.tile([P, PAIR, n_samples], F32, name="samples", align_bytes=DMA_ALIGN)
            nc.sync.dma_start(samples[:], feat_blocks[:, first_block : first_block + PAIR, :])
            if first_block == 0:
                nc.sync.dma_start(offsets[:], offs)
            for k in range(PAIR):
                samples_of.append(samples[:, k, :])
                window = blocks.tile([P, n_classes], F32, name="window", align_bytes=DMA_ALIGN)
                nc.sync.dma_start(window[:], means_blocks[first_block + k])
                windows.append(window)

        for b in range(n_blocks):
            negated = blocks.tile([P, n_samples], F32, name="negated")
            nc.vector.tensor_scalar_mul(negated[:], samples_of[b], -1.0)

            cuts = [0] + [n_samples - (n_samples >> k) for k in range(1, HALVINGS + 1) if b == n_blocks - 1] + [n_samples]
            for first, end in zip(cuts[:-1], cuts[1:]):
                picked = windows[b][:].indirect(offsets[:, first // 16 : end // 16])

                diff = pieces.tile([P, end - first], F32, name="diff")
                nc.vector.tensor_tensor(diff[:], picked, negated[:, first:end], ADD)

                loss = pieces.tile([P, end - first], F32, name="loss", align_bytes=DMA_ALIGN)
                nc.scalar.activation(loss[:], diff[:], SQUARE, scale=math.sqrt(0.5))
                half = n_samples // 2
                for at in range(first, end, half):
                    stop = min(at + half, end)
                    nc.sync.dma_start(out_blocks[b, :, at:stop], loss[:, at - first : stop - first])
